import numpy as np
import ml_dtypes

BF16 = ml_dtypes.bfloat16


def bf(x):
    return np.asarray(x, np.float32).astype(BF16)


def f32(x):
    return np.asarray(x, np.float32)


def f64(x):
    return np.asarray(x).astype(np.float64)


def striped(idx):
    return np.tile(idx.reshape(-1, 16).T, (8, 1))


C, S, N = 128, 256, 512
TEMPERATURE = 0.5
TERMS = 150


def erf(a):
    a = np.asarray(a, np.float64)
    v = np.clip(a, -6.0, 6.0)
    term = v.copy()
    total = v.copy()
    for n in range(1, TERMS):
        term = term * 2.0 * v * v / (2.0 * n + 1.0)
        total = total + term
    return np.where(np.abs(a) > 6.0, np.sign(a), 2.0 / np.sqrt(np.pi) * np.exp(-v * v) * total)


def gelu_erf(v):
    return 0.5 * v * (1.0 + erf(v / np.sqrt(2.0)))


def setup_inputs():
    return {"w1": f32(np.random.standard_normal((C, S))), "b1": f32(0.1 * np.random.standard_normal((C, 1))), "w2": bf(np.random.standard_normal((C, C)) / np.sqrt(C)), "b2": f32(0.1 * np.random.standard_normal((C, 1))), "keys": bf(0.15 * np.random.standard_normal((C, S))), "offs": striped(np.random.permutation(np.tile(np.arange(S), 2))[:N])}


def reference(w1, b1, w2, b2, keys, offs):
    idx = offs[:16].T.reshape(-1)
    h = gelu_erf(f64(w1)[:, idx] + f64(b1))
    q = f64(w2).T @ h + f64(b2)
    z = (q.T @ f64(keys)) / max(abs(TEMPERATURE), 0.1)
    e = np.exp(z)
    return e / e.sum(axis=1, keepdims=True)

@@ -1,0 +1,72 @@
+import concourse.mybir as mybir
+
+F32 = mybir.dt.float32
+BF16 = mybir.dt.bfloat16
+U16 = mybir.dt.uint16
+ADD = mybir.AluOpType.add
+MULT = mybir.AluOpType.mult
+ACT = mybir.ActivationFunctionType
+AXIS_X = mybir.AxisListType.X
+
+C = 128
+S = 256
+N = 512
+PIECE = 256
+ROWS = 128
+INV_TEMPERATURE = 2.0
+
+FLOPS = 2 * C * C * N + 2 * C * N * S
+
+
+def tile_trulyneuraluartv2_kernel(tc, w1, b1, w2, b2, keys, offs, out):
+    nc = tc.nc
+    with (
+        tc.tile_pool(name="held", bufs=1) as held,
+        tc.tile_pool(name="work", bufs=2) as work,
+        tc.tile_pool(name="rows", bufs=4) as rows,
+        tc.psum_pool(name="q_banks", bufs=2) as q_banks,
+        tc.psum_pool(name="z_banks", bufs=4) as z_banks,
+    ):
+        offsets = held.tile([C, N // 16], U16, name="offsets")
+        nc.sync.dma_start(offsets[:], offs)
+        table = held.tile([C, S], F32, name="table")
+        nc.sync.dma_start(table[:], w1)
+        b1_col = held.tile([C, 1], F32, name="b1_col")
+        nc.sync.dma_start(b1_col[:], b1)
+        b1_wide = held.tile([C, PIECE], F32, name="b1_wide")
+        nc.vector.tensor_copy(b1_wide[:], b1_col[:, 0:1].to_broadcast([C, PIECE]))
+        w2_sb = held.tile([C, C], BF16, name="w2_sb")
+        nc.scalar.dma_start(w2_sb[:], w2)
+        b2_col = held.tile([C, 1], F32, name="b2_col")
+        nc.scalar.dma_start(b2_col[:], b2)
+        keys_sb = held.tile([C, S], BF16, name="keys_sb")
+        nc.scalar.dma_start(keys_sb[:], keys)
+
+        for piece in range(N // PIECE):
+            piece_offsets = offsets[:, piece * (PIECE // 16) : (piece + 1) * (PIECE // 16)]
+            pre = work.tile([C, PIECE], F32, name="pre")
+            nc.vector.tensor_tensor(pre[:], table[:].indirect(piece_offsets), b1_wide[:], ADD)
+            h = work.tile([C, PIECE], BF16, name="h")
+            nc.scalar.activation(h[:], pre[:], ACT.Gelu)
+
+            q_ps = q_banks.tile([C, PIECE], F32, name="q_ps")
+            nc.tensor.matmul(q_ps[:], w2_sb[:], h[:], start=True, stop=True)
+            q = work.tile([C, PIECE], BF16, name="q")
+            nc.vector.tensor_scalar(q[:], q_ps[:], b2_col[:, 0:1], INV_TEMPERATURE, ADD, MULT)
+
+            for block in range(PIECE // ROWS):
+                z_ps = z_banks.tile([ROWS, S], F32, name="z_ps")
+                nc.tensor.matmul(
+                    z_ps[:], q[:, block * ROWS : (block + 1) * ROWS], keys_sb[:], start=True, stop=True
+                )
+                neg_max = rows.tile([ROWS, 1], F32, name="neg_max")
+                nc.vector.reduce_max(neg_max[:], z_ps[:], AXIS_X, negate=True)
+                e = rows.tile([ROWS, S], F32, name="e")
+                e_sum = rows.tile([ROWS, 1], F32, name="e_sum")
+                nc.scalar.activation(e[:], z_ps[:], ACT.Exp, bias=neg_max[:, 0:1], accum_out=e_sum[:, 0:1])
+                inv_sum = rows.tile([ROWS, 1], F32, name="inv_sum")
+                nc.vector.reciprocal(inv_sum[:], e_sum[:])
+                probs = rows.tile([ROWS, S], F32, name="probs")
+                nc.vector.tensor_scalar_mul(probs[:], e[:], inv_sum[:, 0:1])
+                first_row = piece * PIECE + block * ROWS
+                nc.sync.dma_start(out[first_row : first_row + ROWS, :], probs[:])

@@ -20,53 +20,63 @@ FLOPS = 2 * C * C * N + 2 * C * N * S
 
 def tile_trulyneuraluartv2_kernel(tc, w1, b1, w2, b2, keys, offs, out):
     nc = tc.nc
+    n_pieces = N // PIECE
+    n_blocks = N // ROWS
     with (
         tc.tile_pool(name="held", bufs=1) as held,
-        tc.tile_pool(name="work", bufs=2) as work,
-        tc.tile_pool(name="rows", bufs=4) as rows,
-        tc.psum_pool(name="q_banks", bufs=2) as q_banks,
-        tc.psum_pool(name="z_banks", bufs=4) as z_banks,
+        tc.tile_pool(name="pieces", bufs=n_pieces) as pieces,
+        tc.tile_pool(name="blocks", bufs=n_blocks) as blocks,
+        tc.psum_pool(name="q_banks", bufs=n_pieces) as q_banks,
+        tc.psum_pool(name="z_banks", bufs=n_blocks) as z_banks,
     ):
         offsets = held.tile([C, N // 16], U16, name="offsets")
         nc.sync.dma_start(offsets[:], offs)
         table = held.tile([C, S], F32, name="table")
-        nc.sync.dma_start(table[:], w1)
+        nc.scalar.dma_start(table[:], w1)
         b1_col = held.tile([C, 1], F32, name="b1_col")
         nc.sync.dma_start(b1_col[:], b1)
-        b1_wide = held.tile([C, PIECE], F32, name="b1_wide")
-        nc.vector.tensor_copy(b1_wide[:], b1_col[:, 0:1].to_broadcast([C, PIECE]))
         w2_sb = held.tile([C, C], BF16, name="w2_sb")
         nc.scalar.dma_start(w2_sb[:], w2)
         b2_col = held.tile([C, 1], F32, name="b2_col")
-        nc.scalar.dma_start(b2_col[:], b2)
+        nc.sync.dma_start(b2_col[:], b2)
         keys_sb = held.tile([C, S], BF16, name="keys_sb")
         nc.scalar.dma_start(keys_sb[:], keys)
 
-        for piece in range(N // PIECE):
+        b1_wide = held.tile([C, PIECE], F32, name="b1_wide")
+        nc.vector.tensor_copy(b1_wide[:], b1_col[:, 0:1].to_broadcast([C, PIECE]))
+
+        h_pieces = []
+        for piece in range(n_pieces):
             piece_offsets = offsets[:, piece * (PIECE // 16) : (piece + 1) * (PIECE // 16)]
-            pre = work.tile([C, PIECE], F32, name="pre")
+            pre = pieces.tile([C, PIECE], F32, name="pre")
             nc.vector.tensor_tensor(pre[:], table[:].indirect(piece_offsets), b1_wide[:], ADD)
-            h = work.tile([C, PIECE], BF16, name="h")
+            h = pieces.tile([C, PIECE], BF16, name="h")
             nc.scalar.activation(h[:], pre[:], ACT.Gelu)
+            h_pieces.append(h)
 
+        z_blocks = []
+        neg_max_blocks = []
+        for piece in range(n_pieces):
             q_ps = q_banks.tile([C, PIECE], F32, name="q_ps")
-            nc.tensor.matmul(q_ps[:], w2_sb[:], h[:], start=True, stop=True)
-            q = work.tile([C, PIECE], BF16, name="q")
+            nc.tensor.matmul(q_ps[:], w2_sb[:], h_pieces[piece][:], start=True, stop=True)
+            q = pieces.tile([C, PIECE], BF16, name="q")
             nc.vector.tensor_scalar(q[:], q_ps[:], b2_col[:, 0:1], INV_TEMPERATURE, ADD, MULT)
-
-            for block in range(PIECE // ROWS):
+            for half in range(PIECE // ROWS):
                 z_ps = z_banks.tile([ROWS, S], F32, name="z_ps")
-                nc.tensor.matmul(
-                    z_ps[:], q[:, block * ROWS : (block + 1) * ROWS], keys_sb[:], start=True, stop=True
-                )
-                neg_max = rows.tile([ROWS, 1], F32, name="neg_max")
+                nc.tensor.matmul(z_ps[:], q[:, half * ROWS : (half + 1) * ROWS], keys_sb[:], start=True, stop=True)
+                neg_max = blocks.tile([ROWS, 1], F32, name="neg_max")
                 nc.vector.reduce_max(neg_max[:], z_ps[:], AXIS_X, negate=True)
-                e = rows.tile([ROWS, S], F32, name="e")
-                e_sum = rows.tile([ROWS, 1], F32, name="e_sum")
-                nc.scalar.activation(e[:], z_ps[:], ACT.Exp, bias=neg_max[:, 0:1], accum_out=e_sum[:, 0:1])
-                inv_sum = rows.tile([ROWS, 1], F32, name="inv_sum")
-                nc.vector.reciprocal(inv_sum[:], e_sum[:])
-                probs = rows.tile([ROWS, S], F32, name="probs")
-                nc.vector.tensor_scalar_mul(probs[:], e[:], inv_sum[:, 0:1])
-                first_row = piece * PIECE + block * ROWS
-                nc.sync.dma_start(out[first_row : first_row + ROWS, :], probs[:])
+                z_blocks.append(z_ps)
+                neg_max_blocks.append(neg_max)
+
+        for block in range(n_blocks):
+            e = blocks.tile([ROWS, S], F32, name="e")
+            e_sum = blocks.tile([ROWS, 1], F32, name="e_sum")
+            nc.scalar.activation(
+                e[:], z_blocks[block][:], ACT.Exp, bias=neg_max_blocks[block][:, 0:1], accum_out=e_sum[:, 0:1]
+            )
+            inv_sum = blocks.tile([ROWS, 1], F32, name="inv_sum")
+            nc.vector.reciprocal(inv_sum[:], e_sum[:])
+            probs = blocks.tile([ROWS, S], F32, name="probs")
+            nc.vector.tensor_scalar_mul(probs[:], e[:], inv_sum[:, 0:1])
+            nc.sync.dma_start(out[block * ROWS : (block + 1) * ROWS, :], probs[:])

@@ -54,20 +54,26 @@ def tile_trulyneuraluartv2_kernel(tc, w1, b1, w2, b2, keys, offs, out):
             nc.scalar.activation(h[:], pre[:], ACT.Gelu)
             h_pieces.append(h)
 
-        z_blocks = []
-        neg_max_blocks = []
+        q_pieces = []
         for piece in range(n_pieces):
             q_ps = q_banks.tile([C, PIECE], F32, name="q_ps")
             nc.tensor.matmul(q_ps[:], w2_sb[:], h_pieces[piece][:], start=True, stop=True)
             q = pieces.tile([C, PIECE], BF16, name="q")
             nc.vector.tensor_scalar(q[:], q_ps[:], b2_col[:, 0:1], INV_TEMPERATURE, ADD, MULT)
-            for half in range(PIECE // ROWS):
-                z_ps = z_banks.tile([ROWS, S], F32, name="z_ps")
-                nc.tensor.matmul(z_ps[:], q[:, half * ROWS : (half + 1) * ROWS], keys_sb[:], start=True, stop=True)
-                neg_max = blocks.tile([ROWS, 1], F32, name="neg_max")
-                nc.vector.reduce_max(neg_max[:], z_ps[:], AXIS_X, negate=True)
-                z_blocks.append(z_ps)
-                neg_max_blocks.append(neg_max)
+            q_pieces.append(q)
+
+        z_blocks = []
+        neg_max_blocks = []
+        for block in range(n_blocks):
+            piece, half = divmod(block, PIECE // ROWS)
+            z_ps = z_banks.tile([ROWS, S], F32, name="z_ps")
+            nc.tensor.matmul(
+                z_ps[:], q_pieces[piece][:, half * ROWS : (half + 1) * ROWS], keys_sb[:], start=True, stop=True
+            )
+            neg_max = blocks.tile([ROWS, 1], F32, name="neg_max")
+            nc.vector.reduce_max(neg_max[:], z_ps[:], AXIS_X, negate=True)
+            z_blocks.append(z_ps)
+            neg_max_blocks.append(neg_max)
 
         for block in range(n_blocks):
             e = blocks.tile([ROWS, S], F32, name="e")

@@ -11,7 +11,7 @@ AXIS_X = mybir.AxisListType.X
 C = 128
 S = 256
 N = 512
-PIECE = 256
+PIECE = 128
 ROWS = 128
 INV_TEMPERATURE = 2.0
 
@@ -54,26 +54,20 @@ def tile_trulyneuraluartv2_kernel(tc, w1, b1, w2, b2, keys, offs, out):
             nc.scalar.activation(h[:], pre[:], ACT.Gelu)
             h_pieces.append(h)
 
-        q_pieces = []
+        z_blocks = []
+        neg_max_blocks = []
         for piece in range(n_pieces):
             q_ps = q_banks.tile([C, PIECE], F32, name="q_ps")
             nc.tensor.matmul(q_ps[:], w2_sb[:], h_pieces[piece][:], start=True, stop=True)
             q = pieces.tile([C, PIECE], BF16, name="q")
             nc.vector.tensor_scalar(q[:], q_ps[:], b2_col[:, 0:1], INV_TEMPERATURE, ADD, MULT)
-            q_pieces.append(q)
-
-        z_blocks = []
-        neg_max_blocks = []
-        for block in range(n_blocks):
-            piece, half = divmod(block, PIECE // ROWS)
-            z_ps = z_banks.tile([ROWS, S], F32, name="z_ps")
-            nc.tensor.matmul(
-                z_ps[:], q_pieces[piece][:, half * ROWS : (half + 1) * ROWS], keys_sb[:], start=True, stop=True
-            )
-            neg_max = blocks.tile([ROWS, 1], F32, name="neg_max")
-            nc.vector.reduce_max(neg_max[:], z_ps[:], AXIS_X, negate=True)
-            z_blocks.append(z_ps)
-            neg_max_blocks.append(neg_max)
+            for half in range(PIECE // ROWS):
+                z_ps = z_banks.tile([ROWS, S], F32, name="z_ps")
+                nc.tensor.matmul(z_ps[:], q[:, half * ROWS : (half + 1) * ROWS], keys_sb[:], start=True, stop=True)
+                neg_max = blocks.tile([ROWS, 1], F32, name="neg_max")
+                nc.vector.reduce_max(neg_max[:], z_ps[:], AXIS_X, negate=True)
+                z_blocks.append(z_ps)
+                neg_max_blocks.append(neg_max)
 
         for block in range(n_blocks):
             e = blocks.tile([ROWS, S], F32, name="e")

@@ -29,12 +29,12 @@ def tile_trulyneuraluartv2_kernel(tc, w1, b1, w2, b2, keys, offs, out):
         tc.psum_pool(name="q_banks", bufs=n_pieces) as q_banks,
         tc.psum_pool(name="z_banks", bufs=n_blocks) as z_banks,
     ):
-        offsets = held.tile([C, N // 16], U16, name="offsets")
-        nc.sync.dma_start(offsets[:], offs)
-        table = held.tile([C, S], F32, name="table")
-        nc.scalar.dma_start(table[:], w1)
         b1_col = held.tile([C, 1], F32, name="b1_col")
         nc.sync.dma_start(b1_col[:], b1)
+        table = held.tile([C, S], F32, name="table")
+        nc.scalar.dma_start(table[:], w1)
+        offsets = held.tile([C, N // 16], U16, name="offsets")
+        nc.sync.dma_start(offsets[:], offs)
         w2_sb = held.tile([C, C], BF16, name="w2_sb")
         nc.scalar.dma_start(w2_sb[:], w2)
         b2_col = held.tile([C, 1], F32, name="b2_col")

@@ -32,15 +32,15 @@ def tile_trulyneuraluartv2_kernel(tc, w1, b1, w2, b2, keys, offs, out):
         b1_col = held.tile([C, 1], F32, name="b1_col")
         nc.sync.dma_start(b1_col[:], b1)
         table = held.tile([C, S], F32, name="table")
-        nc.scalar.dma_start(table[:], w1)
+        nc.sync.dma_start(table[:], w1)
         offsets = held.tile([C, N // 16], U16, name="offsets")
         nc.sync.dma_start(offsets[:], offs)
         w2_sb = held.tile([C, C], BF16, name="w2_sb")
-        nc.scalar.dma_start(w2_sb[:], w2)
+        nc.sync.dma_start(w2_sb[:], w2)
         b2_col = held.tile([C, 1], F32, name="b2_col")
         nc.sync.dma_start(b2_col[:], b2)
         keys_sb = held.tile([C, S], BF16, name="keys_sb")
-        nc.scalar.dma_start(keys_sb[:], keys)
+        nc.sync.dma_start(keys_sb[:], keys)
 
         b1_wide = held.tile([C, PIECE], F32, name="b1_wide")
         nc.vector.tensor_copy(b1_wide[:], b1_col[:, 0:1].to_broadcast([C, PIECE]))

@@ -11,7 +11,8 @@ AXIS_X = mybir.AxisListType.X
 C = 128
 S = 256
 N = 512
-PIECE = 128
+PIECES = (192, 128, 128, 64)
+WIDEST = max(PIECES)
 ROWS = 128
 INV_TEMPERATURE = 2.0
 
@@ -20,7 +21,8 @@ FLOPS = 2 * C * C * N + 2 * C * N * S
 
 def tile_trulyneuraluartv2_kernel(tc, w1, b1, w2, b2, keys, offs, out):
     nc = tc.nc
-    n_pieces = N // PIECE
+    assert sum(PIECES) == N
+    n_pieces = len(PIECES)
     n_blocks = N // ROWS
     with (
         tc.tile_pool(name="held", bufs=1) as held,
@@ -42,28 +44,35 @@ def tile_trulyneuraluartv2_kernel(tc, w1, b1, w2, b2, keys, offs, out):
         keys_sb = held.tile([C, S], BF16, name="keys_sb")
         nc.sync.dma_start(keys_sb[:], keys)
 
-        b1_wide = held.tile([C, PIECE], F32, name="b1_wide")
-        nc.vector.tensor_copy(b1_wide[:], b1_col[:, 0:1].to_broadcast([C, PIECE]))
+        b1_wide = held.tile([C, WIDEST], F32, name="b1_wide")
+        nc.vector.tensor_copy(b1_wide[:], b1_col[:, 0:1].to_broadcast([C, WIDEST]))
 
         h_pieces = []
-        for piece in range(n_pieces):
-            piece_offsets = offsets[:, piece * (PIECE // 16) : (piece + 1) * (PIECE // 16)]
-            pre = pieces.tile([C, PIECE], F32, name="pre")
-            nc.vector.tensor_tensor(pre[:], table[:].indirect(piece_offsets), b1_wide[:], ADD)
-            h = pieces.tile([C, PIECE], BF16, name="h")
-            nc.scalar.activation(h[:], pre[:], ACT.Gelu)
+        first = 0
+        for width in PIECES:
+            piece_offsets = offsets[:, first // 16 : (first + width) // 16]
+            pre = pieces.tile([C, WIDEST], F32, name="pre")
+            nc.vector.tensor_tensor(pre[:, 0:width], table[:].indirect(piece_offsets), b1_wide[:, 0:width], ADD)
+            h = pieces.tile([C, WIDEST], BF16, name="h")
+            nc.scalar.activation(h[:, 0:width], pre[:, 0:width], ACT.Gelu)
             h_pieces.append(h)
+            first += width
 
+        q = held.tile([C, N], BF16, name="q")
         z_blocks = []
         neg_max_blocks = []
-        for piece in range(n_pieces):
-            q_ps = q_banks.tile([C, PIECE], F32, name="q_ps")
-            nc.tensor.matmul(q_ps[:], w2_sb[:], h_pieces[piece][:], start=True, stop=True)
-            q = pieces.tile([C, PIECE], BF16, name="q")
-            nc.vector.tensor_scalar(q[:], q_ps[:], b2_col[:, 0:1], INV_TEMPERATURE, ADD, MULT)
-            for half in range(PIECE // ROWS):
+        first = 0
+        for piece, width in enumerate(PIECES):
+            q_ps = q_banks.tile([C, WIDEST], F32, name="q_ps")
+            nc.tensor.matmul(q_ps[:, 0:width], w2_sb[:], h_pieces[piece][:, 0:width], start=True, stop=True)
+            nc.vector.tensor_scalar(
+                q[:, first : first + width], q_ps[:, 0:width], b2_col[:, 0:1], INV_TEMPERATURE, ADD, MULT
+            )
+            first += width
+            while (len(z_blocks) + 1) * ROWS <= first:
+                block = len(z_blocks)
                 z_ps = z_banks.tile([ROWS, S], F32, name="z_ps")
-                nc.tensor.matmul(z_ps[:], q[:, half * ROWS : (half + 1) * ROWS], keys_sb[:], start=True, stop=True)
+                nc.tensor.matmul(z_ps[:], q[:, block * ROWS : (block + 1) * ROWS], keys_sb[:], start=True, stop=True)
                 neg_max = blocks.tile([ROWS, 1], F32, name="neg_max")
                 nc.vector.reduce_max(neg_max[:], z_ps[:], AXIS_X, negate=True)
                 z_blocks.append(z_ps)

@@ -14,6 +14,7 @@ N = 512
 PIECES = (192, 128, 128, 64)
 WIDEST = max(PIECES)
 ROWS = 128
+DMA_ALIGN = 256
 INV_TEMPERATURE = 2.0
 
 FLOPS = 2 * C * C * N + 2 * C * N * S
@@ -33,15 +34,15 @@ def tile_trulyneuraluartv2_kernel(tc, w1, b1, w2, b2, keys, offs, out):
     ):
         b1_col = held.tile([C, 1], F32, name="b1_col")
         nc.sync.dma_start(b1_col[:], b1)
-        table = held.tile([C, S], F32, name="table")
+        table = held.tile([C, S], F32, name="table", align_bytes=DMA_ALIGN)
         nc.sync.dma_start(table[:], w1)
         offsets = held.tile([C, N // 16], U16, name="offsets")
         nc.sync.dma_start(offsets[:], offs)
-        w2_sb = held.tile([C, C], BF16, name="w2_sb")
+        w2_sb = held.tile([C, C], BF16, name="w2_sb", align_bytes=DMA_ALIGN)
         nc.sync.dma_start(w2_sb[:], w2)
         b2_col = held.tile([C, 1], F32, name="b2_col")
         nc.sync.dma_start(b2_col[:], b2)
-        keys_sb = held.tile([C, S], BF16, name="keys_sb")
+        keys_sb = held.tile([C, S], BF16, name="keys_sb", align_bytes=DMA_ALIGN)
         nc.sync.dma_start(keys_sb[:], keys)
 
         b1_wide = held.tile([C, WIDEST], F32, name="b1_wide")
@@ -86,6 +87,6 @@ def tile_trulyneuraluartv2_kernel(tc, w1, b1, w2, b2, keys, offs, out):
             )
             inv_sum = blocks.tile([ROWS, 1], F32, name="inv_sum")
             nc.vector.reciprocal(inv_sum[:], e_sum[:])
-            probs = blocks.tile([ROWS, S], F32, name="probs")
+            probs = blocks.tile([ROWS, S], F32, name="probs", align_bytes=DMA_ALIGN)
             nc.vector.tensor_scalar_mul(probs[:], e[:], inv_sum[:, 0:1])
             nc.sync.dma_start(out[block * ROWS : (block + 1) * ROWS, :], probs[:])

import concourse.mybir as mybir

F32 = mybir.dt.float32
BF16 = mybir.dt.bfloat16
U16 = mybir.dt.uint16
ADD = mybir.AluOpType.add
MULT = mybir.AluOpType.mult
ACT = mybir.ActivationFunctionType
AXIS_X = mybir.AxisListType.X

C = 128
S = 256
N = 512
PIECES = (192, 128, 128, 64)
WIDEST = max(PIECES)
ROWS = 128
DMA_ALIGN = 256
INV_TEMPERATURE = 2.0

FLOPS = 2 * C * C * N + 2 * C * N * S


def tile_trulyneuraluartv2_kernel(tc, w1, b1, w2, b2, keys, offs, out):
    nc = tc.nc
    assert sum(PIECES) == N
    n_pieces = len(PIECES)
    n_blocks = N // ROWS
    with (
        tc.tile_pool(name="held", bufs=1) as held,
        tc.tile_pool(name="pieces", bufs=n_pieces) as pieces,
        tc.tile_pool(name="blocks", bufs=n_blocks) as blocks,
        tc.psum_pool(name="q_banks", bufs=n_pieces) as q_banks,
        tc.psum_pool(name="z_banks", bufs=n_blocks) as z_banks,
    ):
        b1_col = held.tile([C, 1], F32, name="b1_col")
        nc.sync.dma_start(b1_col[:], b1)
        table = held.tile([C, S], F32, name="table", align_bytes=DMA_ALIGN)
        nc.sync.dma_start(table[:], w1)
        offsets = held.tile([C, N // 16], U16, name="offsets")
        nc.sync.dma_start(offsets[:], offs)
        w2_sb = held.tile([C, C], BF16, name="w2_sb", align_bytes=DMA_ALIGN)
        nc.sync.dma_start(w2_sb[:], w2)
        b2_col = held.tile([C, 1], F32, name="b2_col")
        nc.sync.dma_start(b2_col[:], b2)
        keys_sb = held.tile([C, S], BF16, name="keys_sb", align_bytes=DMA_ALIGN)
        nc.sync.dma_start(keys_sb[:], keys)

        b1_wide = held.tile([C, WIDEST], F32, name="b1_wide")
        nc.vector.tensor_copy(b1_wide[:], b1_col[:, 0:1].to_broadcast([C, WIDEST]))

        h_pieces = []
        first = 0
        for width in PIECES:
            piece_offsets = offsets[:, first // 16 : (first + width) // 16]
            pre = pieces.tile([C, WIDEST], F32, name="pre")
            nc.vector.tensor_tensor(pre[:, 0:width], table[:].indirect(piece_offsets), b1_wide[:, 0:width], ADD)
            h = pieces.tile([C, WIDEST], BF16, name="h")
            nc.scalar.activation(h[:, 0:width], pre[:, 0:width], ACT.Gelu)
            h_pieces.append(h)
            first += width

        q = held.tile([C, N], BF16, name="q")
        z_blocks = []
        neg_max_blocks = []
        first = 0
        for piece, width in enumerate(PIECES):
            q_ps = q_banks.tile([C, WIDEST], F32, name="q_ps")
            nc.tensor.matmul(q_ps[:, 0:width], w2_sb[:], h_pieces[piece][:, 0:width], start=True, stop=True)
            nc.vector.tensor_scalar(
                q[:, first : first + width], q_ps[:, 0:width], b2_col[:, 0:1], INV_TEMPERATURE, ADD, MULT
            )
            first += width
            while (len(z_blocks) + 1) * ROWS <= first:
                block = len(z_blocks)
                z_ps = z_banks.tile([ROWS, S], F32, name="z_ps")
                nc.tensor.matmul(z_ps[:], q[:, block * ROWS : (block + 1) * ROWS], keys_sb[:], start=True, stop=True)
                neg_max = blocks.tile([ROWS, 1], F32, name="neg_max")
                nc.vector.reduce_max(neg_max[:], z_ps[:], AXIS_X, negate=True)
                z_blocks.append(z_ps)
                neg_max_blocks.append(neg_max)

        for block in range(n_blocks):
            e = blocks.tile([ROWS, S], F32, name="e")
            e_sum = blocks.tile([ROWS, 1], F32, name="e_sum")
            nc.scalar.activation(
                e[:], z_blocks[block][:], ACT.Exp, bias=neg_max_blocks[block][:, 0:1], accum_out=e_sum[:, 0:1]
            )
            inv_sum = blocks.tile([ROWS, 1], F32, name="inv_sum")
            nc.vector.reciprocal(inv_sum[:], e_sum[:])
            probs = blocks.tile([ROWS, S], F32, name="probs", align_bytes=DMA_ALIGN)
            nc.vector.tensor_scalar_mul(probs[:], e[:], inv_sum[:, 0:1])
            nc.sync.dma_start(out[block * ROWS : (block + 1) * ROWS, :], probs[:])
